import numpy as np
import ml_dtypes


def mxq(x, axis, fmt="e4m3"):
    dtype, down = {"e4m3": (ml_dtypes.float8_e4m3fn, 7), "e5m2": (ml_dtypes.float8_e5m2, 14)}[fmt]
    v = np.moveaxis(np.asarray(x, np.float32).astype(ml_dtypes.bfloat16).astype(np.float64), axis, -1)
    blocks = v.reshape(v.shape[:-1] + (-1, 32))
    amax = np.abs(blocks).max(-1, keepdims=True)
    byte = np.maximum(np.where(amax > 0, np.frexp(amax)[1] - 1 + 127, 0) - down, 1)
    scale = np.exp2(byte - 127.0)
    codes = (blocks / scale).astype(np.float32).astype(dtype).astype(np.float64)
    return np.moveaxis((codes * scale).reshape(v.shape), -1, axis)


WIDE = False


def mx_kscale(k):
    if not WIDE:
        return np.ones(k)
    levels = np.array([10, -10, 5, -5, 0])
    a = np.random.permutation(np.resize(levels, k // 512 * 4)).reshape(k // 512, 4)
    idx = np.arange(k)
    return np.exp2(a[idx // 512, idx % 128 // 32])


BF16 = ml_dtypes.bfloat16


def bf(x):
    return np.asarray(x, np.float32).astype(BF16)


def f64(x):
    return np.asarray(x).astype(np.float64)


E2M1 = np.array([0.0, 0.5, 1.0, 1.5, 2.0, 3.0, 4.0, 6.0, -0.0, -0.5, -1.0, -1.5, -2.0, -3.0, -4.0, -6.0])


def pack_weight(w, fmt):
    k, n = w.shape
    w = f64(bf(w)).reshape(k // 32, 32, n)
    amax = np.abs(w).max(1)
    if fmt == "e4m3":
        byte = np.frexp(amax)[1] - 1 + 127 - 7
    else:
        mant, ex = np.frexp(amax / 6.0)
        byte = np.where(mant > 0.5, ex, ex - 1) + 127
    byte = np.clip(np.where(amax > 0, byte, 1), 1, 254)
    scaled = (w * np.exp2(127.0 - byte)[:, None, :]).reshape(k, n).astype(np.float32)
    by_word = np.ascontiguousarray(scaled.reshape(k // 512, 128, 4, n).transpose(0, 1, 3, 2))
    if fmt == "e4m3":
        words = by_word.astype(ml_dtypes.float8_e4m3fn).view(np.uint8)
    else:
        c = by_word.astype(ml_dtypes.float4_e2m1fn).view(np.uint8) & 0xF
        words = c[..., 0::2] | (c[..., 1::2] << 4)
    return np.ascontiguousarray(words), np.ascontiguousarray(byte.astype(np.uint8).reshape(k // 512, 16, n))


def unpack_weight(words, scales, fmt):
    g, p, n, _ = words.shape
    if fmt == "e4m3":
        vals = np.ascontiguousarray(words).view(ml_dtypes.float8_e4m3fn).astype(np.float64)
    else:
        nib = np.empty((g, p, n, 4), np.uint8)
        nib[..., 0::2] = words & 0xF
        nib[..., 1::2] = words >> 4
        vals = E2M1[nib]
    vals = vals * np.repeat(np.exp2(scales.astype(np.float64) - 127.0), 8, axis=1)[..., None]
    return vals.transpose(0, 1, 3, 2).reshape(g * 512, n)

def pack4(w):
    words, scales = pack_weight(w, "e2m1")
    return words.reshape(words.shape[0], 128, -1), scales


def unpack4(words, scales):
    return unpack_weight(words.reshape(words.shape[0], 128, -1, 2), scales, "e2m1")


B, S, D, DM, DK = 2, 512, 1024, 1024, 64
LN_EPS = 1e-5


def setup_inputs():
    s = mx_kscale(DM)
    h_attn = bf(np.random.standard_normal((B, S, DM)) * 0.3 * s)
    Wo_words, Wo_scales = pack4(np.random.standard_normal((DM, D)) * 3.0 / np.sqrt(DM) / s[:, None])
    return {
        "h_attn": h_attn,
        "Wo_words": Wo_words,
        "Wo_scales": Wo_scales,
        "bo": bf(np.random.standard_normal((B, S, D)) * 0.5 + np.random.uniform(0.25, 0.75, (B, 1, 1))),
        "x": bf(np.random.standard_normal((B, S, D))),
        "gamma": bf(1.0 + 0.1 * np.random.standard_normal((S, D))),
        "beta": bf(0.1 * np.random.standard_normal((S, D))),
    }


def reference(h_attn, Wo_words, Wo_scales, bo, x, gamma, beta):
    o = (mxq(f64(h_attn), 2, "e4m3") @ unpack4(Wo_words, Wo_scales)) + f64(bo)
    o = o + f64(x)
    mu = o.mean(axis=(-2, -1), keepdims=True)
    var = np.square(o - mu).mean(axis=(-2, -1), keepdims=True)
    return (o - mu) / np.sqrt(var + LN_EPS) * f64(gamma) + f64(beta)

@@ -1,0 +1,229 @@
+import concourse.mybir as mybir
+from concourse.masks import make_identity
+
+F32 = mybir.dt.float32
+BF16 = mybir.dt.bfloat16
+I32 = mybir.dt.int32
+U32 = mybir.dt.uint32
+U8 = mybir.dt.uint8
+FP8X4 = mybir.dt.float8_e4m3fn_x4
+FP4X4 = mybir.dt.float4_e2m1fn_x4
+ALU = mybir.AluOpType
+FUNC = mybir.ActivationFunctionType
+
+P = 128
+BATCH = 2
+SEQ = 512
+K = 1024
+N = 1024
+LN_EPS = 1e-5
+
+PACK = 4
+K_PASS = P * PACK
+PASSES = K // K_PASS
+PAIRS = PACK // 2
+WORDS_PER_PASS = K_PASS // 2
+
+TILES_PER_BATCH = SEQ // P
+TILES = BATCH * TILES_PER_BATCH
+BANK = 512
+HALVES = N // BANK
+
+FLOPS = 2 * BATCH * SEQ * K * N
+
+
+def tile_multiheadattn_pb_kernel(tc, h_attn, Wo_words, Wo_scales, bo, x, gamma, beta, out):
+    nc = tc.nc
+
+    h_view = h_attn.rearrange("b (p t) k -> p b t k", t=TILES_PER_BATCH)
+    bo_view = bo.rearrange("b (p t) n -> p b t n", t=TILES_PER_BATCH)
+    x_view = x.rearrange("b (p t) n -> p b t n", t=TILES_PER_BATCH)
+    out_view = out.rearrange("b (p t) n -> p b t n", t=TILES_PER_BATCH)
+
+    def of_tile(view, i):
+        return view[:, i // TILES_PER_BATCH, i % TILES_PER_BATCH, :]
+
+    gamma_view = gamma.rearrange("(p t) n -> p t n", t=TILES_PER_BATCH)
+    beta_view = beta.rearrange("(p t) n -> p t n", t=TILES_PER_BATCH)
+
+    with (
+        tc.tile_pool(name="keep", bufs=1) as keep,
+        tc.psum_pool(name="psum_t", bufs=2) as psum_t,
+        tc.psum_pool(name="psum_acc", bufs=4) as psum_acc,
+        tc.psum_pool(name="psum_stat", bufs=1) as psum_stat,
+        tc.manual_schedule(),
+    ):
+        h_sb = keep.tile([P, TILES, K], BF16)
+        bo_sb = keep.tile([P, TILES, N], BF16)
+        x_sb = keep.tile([P, TILES, N], BF16)
+        gamma_sb = keep.tile([P, TILES_PER_BATCH, N], BF16)
+        beta_sb = keep.tile([P, TILES_PER_BATCH, N], BF16)
+        w_words = keep.tile([P, PASSES, 2 * N], U8, align_bytes=64)
+        w_scales = keep.tile([P, PASSES, N], U8, align_bytes=64)
+        grouped = keep.tile([P, TILES, PASSES, P, PACK], BF16, align_bytes=64)
+        h_codes = keep.tile([P, TILES, PASSES, P], U32, align_bytes=64)
+        h_scales = keep.tile([P, TILES, PASSES, P], U8, align_bytes=64)
+        o_sb = keep.tile([P, TILES, N], F32)
+        y_sb = keep.tile([P, TILES, N], F32)
+        squares = keep.tile([P, N], BF16)
+        identity = keep.tile([P, P], F32)
+        averager = keep.tile([P, P], F32)
+        eps = keep.tile([P, 1], F32)
+        table_warmer = keep.tile([P, 1], F32)
+        o_sums = keep.tile([P, TILES * HALVES], F32)
+        sq_sums = keep.tile([P, TILES], F32)
+        spread = keep.tile([P, TILES_PER_BATCH * HALVES], F32)
+        mean = keep.tile([P, BATCH], F32)
+        var = keep.tile([P, BATCH], F32)
+        rstd = keep.tile([P, BATCH], F32)
+
+        nc.vector.memset(w_scales[:].bitcast(I32), 0)
+        nc.vector.memset(eps[:], LN_EPS)
+        nc.vector.memset(averager[:], 1.0 / (SEQ * N))
+        make_identity(nc, identity[:])
+        nc.scalar.activation(out=table_warmer[:], in_=eps[:], func=FUNC.Abs_reciprocal_sqrt)
+
+        def load_h(i):
+            nc.sync.dma_start(out=h_sb[:, i, :], in_=of_tile(h_view, i))
+
+        def load_bias_and_residual(i):
+            nc.sync.dma_start(out=bo_sb[:, i, :], in_=of_tile(bo_view, i))
+            nc.sync.dma_start(out=x_sb[:, i, :], in_=of_tile(x_view, i))
+
+        load_h(0)
+        nc.sync.dma_start(out=w_words[:].bitcast(I32), in_=Wo_words.bitcast(I32).rearrange("g p c -> p g c"))
+        scale_rows = Wo_scales.bitcast(I32).rearrange("g (q r) c -> r q g c", r=4)
+        for r in range(4):
+            nc.sync.dma_start(out=w_scales[r:P:32, :, :].bitcast(I32), in_=scale_rows[r])
+        for i in range(TILES):
+            if i + 1 < TILES:
+                load_h(i + 1)
+            load_bias_and_residual(i)
+        nc.sync.dma_start(out=gamma_sb[:], in_=gamma_view)
+        nc.sync.dma_start(out=beta_sb[:], in_=beta_view)
+
+        def transpose_and_regroup(i):
+            h_f32 = h_sb[:, i, :].bitcast(F32)
+            flipped = psum_t.tile([P, PASSES, PAIRS, P], F32)
+            for g in range(PASSES):
+                for u in range(PAIRS):
+                    first = g * WORDS_PER_PASS + u
+                    nc.tensor.transpose(
+                        flipped[:, g, u, :], h_f32[:, first : (g + 1) * WORDS_PER_PASS : PAIRS], identity[:]
+                    )
+            nc.scalar.copy(out=grouped[:, i].bitcast(F32), in_=flipped[:].rearrange("p g u m -> p g m u"))
+
+        def quantise(i):
+            nc.vector.quantize_mx(
+                out=h_codes[:, i].rearrange("p g m -> p (g m)").bitcast(FP8X4),
+                scales=h_scales[:, i].rearrange("p g m -> p (g m)"),
+                in_=grouped[:, i].rearrange("p g m j -> p (g m j)"),
+            )
+
+        product = {}
+
+        def project(i):
+            for half in range(HALVES):
+                acc = psum_acc.tile([P, BANK], F32)
+                for g in range(PASSES):
+                    nc.tensor.matmul_mx(
+                        out=acc[:],
+                        lhsT=h_codes[:, i, g, :].bitcast(FP8X4),
+                        lhsT_scale=h_scales[:, i, g, :],
+                        rhs=w_words[:, g, 2 * BANK * half : 2 * BANK * (half + 1)].bitcast(FP4X4),
+                        rhs_scale=w_scales[:, g, BANK * half : BANK * (half + 1)],
+                        start=(g == 0),
+                        stop=(g == PASSES - 1),
+                    )
+                product[i, half] = acc
+
+        def add_bias_and_residual(i):
+            nc.vector.tensor_tensor(out=o_sb[:, i, :], in0=bo_sb[:, i, :], in1=x_sb[:, i, :], op=ALU.add)
+
+        def add_product(i):
+            for half in range(HALVES):
+                cols = slice(BANK * half, BANK * (half + 1))
+                column = HALVES * i + half
+                nc.vector.scalar_tensor_tensor(
+                    out=o_sb[:, i, cols],
+                    in0=product[i, half][:],
+                    scalar=1.0,
+                    in1=o_sb[:, i, cols],
+                    op0=ALU.mult,
+                    op1=ALU.add,
+                    accum_out=o_sums[:, column : column + 1],
+                )
+
+        def average(row_sums, result):
+            columns = row_sums.shape[1]
+            summed = psum_stat.tile([P, TILES_PER_BATCH * HALVES], F32)
+            nc.tensor.matmul(summed[:, :columns], lhsT=averager[:], rhs=row_sums, start=True, stop=True)
+            nc.scalar.activation(
+                out=spread[:, :columns], in_=summed[:, :columns], func=FUNC.Identity, accum_out=result
+            )
+
+        def take_mean(b):
+            per_batch = TILES_PER_BATCH * HALVES
+            average(o_sums[:, per_batch * b : per_batch * (b + 1)], mean[:, b : b + 1])
+
+        def sum_squares(i):
+            b = i // TILES_PER_BATCH
+            nc.scalar.activation(
+                out=squares[:],
+                in_=o_sb[:, i, :],
+                func=FUNC.Square,
+                scale=-1.0,
+                bias=mean[:, b : b + 1],
+                accum_out=sq_sums[:, i : i + 1],
+            )
+
+        def take_rstd(b):
+            average(sq_sums[:, TILES_PER_BATCH * b : TILES_PER_BATCH * (b + 1)], var[:, b : b + 1])
+            nc.scalar.activation(
+                out=rstd[:, b : b + 1], in_=var[:, b : b + 1], func=FUNC.Abs_reciprocal_sqrt, bias=eps[:]
+            )
+
+        for i in range(3):
+            transpose_and_regroup(i)
+        quantise(0)
+        quantise(1)
+        project(0)
+        for step in range(TILES + TILES_PER_BATCH):
+            late = step - TILES_PER_BATCH
+            if late >= 0:
+                sum_squares(late)
+                if late % TILES_PER_BATCH == TILES_PER_BATCH - 1:
+                    take_rstd(late // TILES_PER_BATCH)
+            if step < TILES:
+                if step + 3 < TILES:
+                    transpose_and_regroup(step + 3)
+                if step + 1 < TILES:
+                    project(step + 1)
+                add_bias_and_residual(step)
+                add_product(step)
+                if step + 2 < TILES:
+                    quantise(step + 2)
+                if step % TILES_PER_BATCH == TILES_PER_BATCH - 1:
+                    take_mean(step // TILES_PER_BATCH)
+
+        for b in range(BATCH):
+            tiles = slice(TILES_PER_BATCH * b, TILES_PER_BATCH * (b + 1))
+            nc.vector.scalar_tensor_tensor(
+                out=y_sb[:, tiles, :],
+                in0=o_sb[:, tiles, :],
+                scalar=mean[:, b : b + 1],
+                in1=gamma_sb[:],
+                op0=ALU.subtract,
+                op1=ALU.mult,
+            )
+            for t in range(TILES_PER_BATCH):
+                i = TILES_PER_BATCH * b + t
+                nc.vector.scalar_tensor_tensor(
+                    out=y_sb[:, i, :],
+                    in0=y_sb[:, i, :],
+                    scalar=rstd[:, b : b + 1],
+                    in1=beta_sb[:, t, :],
+                    op0=ALU.mult,
+                    op1=ALU.add,
+                )
+                nc.sync.dma_start(out=of_tile(out_view, i), in_=y_sb[:, i, :])

@@ -29,6 +29,11 @@ TILES = BATCH * TILES_PER_BATCH
 BANK = 512
 HALVES = N // BANK
 
+TENSOR_SUMMED = 3
+
+CENTRE_LAG = TILES_PER_BATCH
+FINISH_LAG = 2 * TILES_PER_BATCH
+
 FLOPS = 2 * BATCH * SEQ * K * N
 
 
@@ -39,17 +44,23 @@ def tile_multiheadattn_pb_kernel(tc, h_attn, Wo_words, Wo_scales, bo, x, gamma, 
     bo_view = bo.rearrange("b (p t) n -> p b t n", t=TILES_PER_BATCH)
     x_view = x.rearrange("b (p t) n -> p b t n", t=TILES_PER_BATCH)
     out_view = out.rearrange("b (p t) n -> p b t n", t=TILES_PER_BATCH)
+    gamma_view = gamma.rearrange("(p t) n -> p t n", t=TILES_PER_BATCH)
+    beta_view = beta.rearrange("(p t) n -> p t n", t=TILES_PER_BATCH)
 
     def of_tile(view, i):
         return view[:, i // TILES_PER_BATCH, i % TILES_PER_BATCH, :]
 
-    gamma_view = gamma.rearrange("(p t) n -> p t n", t=TILES_PER_BATCH)
-    beta_view = beta.rearrange("(p t) n -> p t n", t=TILES_PER_BATCH)
+    def summed_by_tensor(i):
+        return i >= TILES - TENSOR_SUMMED
+
+    def last_of_batch(i):
+        return i % TILES_PER_BATCH == TILES_PER_BATCH - 1
 
     with (
         tc.tile_pool(name="keep", bufs=1) as keep,
-        tc.psum_pool(name="psum_t", bufs=2) as psum_t,
+        tc.psum_pool(name="psum_flip", bufs=1) as psum_flip,
         tc.psum_pool(name="psum_acc", bufs=4) as psum_acc,
+        tc.psum_pool(name="psum_sum", bufs=2) as psum_sum,
         tc.psum_pool(name="psum_stat", bufs=1) as psum_stat,
         tc.manual_schedule(),
     ):
@@ -65,8 +76,9 @@ def tile_multiheadattn_pb_kernel(tc, h_attn, Wo_words, Wo_scales, bo, x, gamma, 
         h_scales = keep.tile([P, TILES, PASSES, P], U8, align_bytes=64)
         o_sb = keep.tile([P, TILES, N], F32)
         y_sb = keep.tile([P, TILES, N], F32)
-        squares = keep.tile([P, N], BF16)
+        unread = keep.tile([P, N], BF16)
         identity = keep.tile([P, P], F32)
+        identity_bf = keep.tile([P, P], BF16)
         averager = keep.tile([P, P], F32)
         eps = keep.tile([P, 1], F32)
         table_warmer = keep.tile([P, 1], F32)
@@ -81,6 +93,7 @@ def tile_multiheadattn_pb_kernel(tc, h_attn, Wo_words, Wo_scales, bo, x, gamma, 
         nc.vector.memset(eps[:], LN_EPS)
         nc.vector.memset(averager[:], 1.0 / (SEQ * N))
         make_identity(nc, identity[:])
+        make_identity(nc, identity_bf[:])
         nc.scalar.activation(out=table_warmer[:], in_=eps[:], func=FUNC.Abs_reciprocal_sqrt)
 
         def load_h(i):
@@ -90,8 +103,15 @@ def tile_multiheadattn_pb_kernel(tc, h_attn, Wo_words, Wo_scales, bo, x, gamma, 
             nc.sync.dma_start(out=bo_sb[:, i, :], in_=of_tile(bo_view, i))
             nc.sync.dma_start(out=x_sb[:, i, :], in_=of_tile(x_view, i))
 
+        def load_w_words(half):
+            words = slice(BANK // 2 * half, BANK // 2 * (half + 1))
+            nc.sync.dma_start(
+                out=w_words[:].bitcast(I32)[:, :, words],
+                in_=Wo_words.bitcast(I32).rearrange("g p c -> p g c")[:, :, words],
+            )
+
         load_h(0)
-        nc.sync.dma_start(out=w_words[:].bitcast(I32), in_=Wo_words.bitcast(I32).rearrange("g p c -> p g c"))
+        load_w_words(0)
         scale_rows = Wo_scales.bitcast(I32).rearrange("g (q r) c -> r q g c", r=4)
         for r in range(4):
             nc.sync.dma_start(out=w_scales[r:P:32, :, :].bitcast(I32), in_=scale_rows[r])
@@ -99,12 +119,15 @@ def tile_multiheadattn_pb_kernel(tc, h_attn, Wo_words, Wo_scales, bo, x, gamma, 
             if i + 1 < TILES:
                 load_h(i + 1)
             load_bias_and_residual(i)
-        nc.sync.dma_start(out=gamma_sb[:], in_=gamma_view)
+            if i == 0:
+                load_w_words(1)
+            if i == CENTRE_LAG + 1:
+                nc.sync.dma_start(out=gamma_sb[:], in_=gamma_view)
         nc.sync.dma_start(out=beta_sb[:], in_=beta_view)
 
         def transpose_and_regroup(i):
             h_f32 = h_sb[:, i, :].bitcast(F32)
-            flipped = psum_t.tile([P, PASSES, PAIRS, P], F32)
+            flipped = psum_flip.tile([P, PASSES, PAIRS, P], F32)
             for g in range(PASSES):
                 for u in range(PAIRS):
                     first = g * WORDS_PER_PASS + u
@@ -140,6 +163,14 @@ def tile_multiheadattn_pb_kernel(tc, h_attn, Wo_words, Wo_scales, bo, x, gamma, 
         def add_bias_and_residual(i):
             nc.vector.tensor_tensor(out=o_sb[:, i, :], in0=bo_sb[:, i, :], in1=x_sb[:, i, :], op=ALU.add)
 
+        def add_bias_and_residual_on_tensor(i):
+            for half in range(HALVES):
+                cols = slice(BANK * half, BANK * (half + 1))
+                both = psum_sum.tile([P, BANK], F32)
+                nc.tensor.matmul(both[:], lhsT=identity_bf[:], rhs=bo_sb[:, i, cols], start=True, stop=False)
+                nc.tensor.matmul(both[:], lhsT=identity_bf[:], rhs=x_sb[:, i, cols], start=False, stop=True)
+                nc.scalar.copy(out=o_sb[:, i, cols], in_=both[:])
+
         def add_product(i):
             for half in range(HALVES):
                 cols = slice(BANK * half, BANK * (half + 1))
@@ -169,7 +200,7 @@ def tile_multiheadattn_pb_kernel(tc, h_attn, Wo_words, Wo_scales, bo, x, gamma, 
         def sum_squares(i):
             b = i // TILES_PER_BATCH
             nc.scalar.activation(
-                out=squares[:],
+                out=unread[:],
                 in_=o_sb[:, i, :],
                 func=FUNC.Square,
                 scale=-1.0,
@@ -183,47 +214,55 @@ def tile_multiheadattn_pb_kernel(tc, h_attn, Wo_words, Wo_scales, bo, x, gamma, 
                 out=rstd[:, b : b + 1], in_=var[:, b : b + 1], func=FUNC.Abs_reciprocal_sqrt, bias=eps[:]
             )
 
-        for i in range(3):
-            transpose_and_regroup(i)
-        quantise(0)
-        quantise(1)
-        project(0)
-        for step in range(TILES + TILES_PER_BATCH):
-            late = step - TILES_PER_BATCH
-            if late >= 0:
-                sum_squares(late)
-                if late % TILES_PER_BATCH == TILES_PER_BATCH - 1:
-                    take_rstd(late // TILES_PER_BATCH)
-            if step < TILES:
-                if step + 3 < TILES:
-                    transpose_and_regroup(step + 3)
-                if step + 1 < TILES:
-                    project(step + 1)
-                add_bias_and_residual(step)
-                add_product(step)
-                if step + 2 < TILES:
-                    quantise(step + 2)
-                if step % TILES_PER_BATCH == TILES_PER_BATCH - 1:
-                    take_mean(step // TILES_PER_BATCH)
-
-        for b in range(BATCH):
-            tiles = slice(TILES_PER_BATCH * b, TILES_PER_BATCH * (b + 1))
+        def centre_and_gain(i):
+            b = i // TILES_PER_BATCH
             nc.vector.scalar_tensor_tensor(
-                out=y_sb[:, tiles, :],
-                in0=o_sb[:, tiles, :],
+                out=y_sb[:, i, :],
+                in0=o_sb[:, i, :],
                 scalar=mean[:, b : b + 1],
-                in1=gamma_sb[:],
+                in1=gamma_sb[:, i % TILES_PER_BATCH, :],
                 op0=ALU.subtract,
                 op1=ALU.mult,
             )
-            for t in range(TILES_PER_BATCH):
-                i = TILES_PER_BATCH * b + t
-                nc.vector.scalar_tensor_tensor(
-                    out=y_sb[:, i, :],
-                    in0=y_sb[:, i, :],
-                    scalar=rstd[:, b : b + 1],
-                    in1=beta_sb[:, t, :],
-                    op0=ALU.mult,
-                    op1=ALU.add,
-                )
-                nc.sync.dma_start(out=of_tile(out_view, i), in_=y_sb[:, i, :])
+
+        def scale_shift_and_store(i):
+            b = i // TILES_PER_BATCH
+            nc.vector.scalar_tensor_tensor(
+                out=y_sb[:, i, :],
+                in0=y_sb[:, i, :],
+                scalar=rstd[:, b : b + 1],
+                in1=beta_sb[:, i % TILES_PER_BATCH, :],
+                op0=ALU.mult,
+                op1=ALU.add,
+            )
+            nc.sync.dma_start(out=of_tile(out_view, i), in_=y_sb[:, i, :])
+
+        transpose_and_regroup(0)
+        transpose_and_regroup(1)
+        quantise(0)
+        project(0)
+        for step in range(TILES + FINISH_LAG):
+            centred = step - CENTRE_LAG
+            finished = step - FINISH_LAG
+            if 0 <= centred < TILES:
+                sum_squares(centred)
+                if last_of_batch(centred):
+                    take_rstd(centred // TILES_PER_BATCH)
+            if step < TILES:
+                if not summed_by_tensor(step):
+                    add_bias_and_residual(step)
+                if step + 1 < TILES:
+                    quantise(step + 1)
+                if step + 2 < TILES:
+                    transpose_and_regroup(step + 2)
+                if step + 1 < TILES:
+                    if summed_by_tensor(step + 1):
+                        add_bias_and_residual_on_tensor(step + 1)
+                    project(step + 1)
+                add_product(step)
+                if last_of_batch(step):
+                    take_mean(step // TILES_PER_BATCH)
+            if 0 <= finished < TILES:
+                scale_shift_and_store(finished)
+            if 0 <= centred < TILES:
+                centre_and_gain(centred)

@@ -29,10 +29,13 @@ TILES = BATCH * TILES_PER_BATCH
 BANK = 512
 HALVES = N // BANK
 
-TENSOR_SUMMED = 3
+TENSOR_SUMMED = 0
 
-CENTRE_LAG = TILES_PER_BATCH
-FINISH_LAG = 2 * TILES_PER_BATCH
+GAMMA_AFTER = 5
+BETA_AFTER = 7
+
+G_TILES = (2, 3)
+GPSIMD_SUMMED = (3, 4, 5, 6, 7)
 
 FLOPS = 2 * BATCH * SEQ * K * N
 
@@ -50,17 +53,16 @@ def tile_multiheadattn_pb_kernel(tc, h_attn, Wo_words, Wo_scales, bo, x, gamma, 
     def of_tile(view, i):
         return view[:, i // TILES_PER_BATCH, i % TILES_PER_BATCH, :]
 
-    def summed_by_tensor(i):
-        return i >= TILES - TENSOR_SUMMED
+    def first_of_batch(i):
+        return i % TILES_PER_BATCH == 0
 
     def last_of_batch(i):
         return i % TILES_PER_BATCH == TILES_PER_BATCH - 1
 
     with (
         tc.tile_pool(name="keep", bufs=1) as keep,
-        tc.psum_pool(name="psum_flip", bufs=1) as psum_flip,
+        tc.psum_pool(name="psum_flip", bufs=2) as psum_flip,
         tc.psum_pool(name="psum_acc", bufs=4) as psum_acc,
-        tc.psum_pool(name="psum_sum", bufs=2) as psum_sum,
         tc.psum_pool(name="psum_stat", bufs=1) as psum_stat,
         tc.manual_schedule(),
     ):
@@ -78,23 +80,24 @@ def tile_multiheadattn_pb_kernel(tc, h_attn, Wo_words, Wo_scales, bo, x, gamma, 
         y_sb = keep.tile([P, TILES, N], F32)
         unread = keep.tile([P, N], BF16)
         identity = keep.tile([P, P], F32)
-        identity_bf = keep.tile([P, P], BF16)
         averager = keep.tile([P, P], F32)
-        eps = keep.tile([P, 1], F32)
+        eps_quarter = keep.tile([P, 1], F32)
         table_warmer = keep.tile([P, 1], F32)
         o_sums = keep.tile([P, TILES * HALVES], F32)
         sq_sums = keep.tile([P, TILES], F32)
         spread = keep.tile([P, TILES_PER_BATCH * HALVES], F32)
-        mean = keep.tile([P, BATCH], F32)
-        var = keep.tile([P, BATCH], F32)
+        shift = keep.tile([P, BATCH], F32)
+        negmean = keep.tile([P, BATCH], F32)
+        e2eps = keep.tile([P, BATCH], F32)
+        dsq = keep.tile([P, BATCH], F32)
         rstd = keep.tile([P, BATCH], F32)
+        nmr = keep.tile([P, BATCH], F32)
 
         nc.vector.memset(w_scales[:].bitcast(I32), 0)
-        nc.vector.memset(eps[:], LN_EPS)
+        nc.vector.memset(eps_quarter[:], LN_EPS / TILES_PER_BATCH)
         nc.vector.memset(averager[:], 1.0 / (SEQ * N))
         make_identity(nc, identity[:])
-        make_identity(nc, identity_bf[:])
-        nc.scalar.activation(out=table_warmer[:], in_=eps[:], func=FUNC.Abs_reciprocal_sqrt)
+        nc.scalar.activation(out=table_warmer[:], in_=eps_quarter[:], func=FUNC.Abs_reciprocal_sqrt)
 
         def load_h(i):
             nc.sync.dma_start(out=h_sb[:, i, :], in_=of_tile(h_view, i))
@@ -118,12 +121,13 @@ def tile_multiheadattn_pb_kernel(tc, h_attn, Wo_words, Wo_scales, bo, x, gamma, 
         for i in range(TILES):
             if i + 1 < TILES:
                 load_h(i + 1)
+            if i == GAMMA_AFTER + 1:
+                nc.sync.dma_start(out=gamma_sb[:], in_=gamma_view)
             load_bias_and_residual(i)
             if i == 0:
                 load_w_words(1)
-            if i == CENTRE_LAG + 1:
-                nc.sync.dma_start(out=gamma_sb[:], in_=gamma_view)
-        nc.sync.dma_start(out=beta_sb[:], in_=beta_view)
+            if i == BETA_AFTER:
+                nc.sync.dma_start(out=beta_sb[:], in_=beta_view)
 
         def transpose_and_regroup(i):
             h_f32 = h_sb[:, i, :].bitcast(F32)
@@ -163,14 +167,6 @@ def tile_multiheadattn_pb_kernel(tc, h_attn, Wo_words, Wo_scales, bo, x, gamma, 
         def add_bias_and_residual(i):
             nc.vector.tensor_tensor(out=o_sb[:, i, :], in0=bo_sb[:, i, :], in1=x_sb[:, i, :], op=ALU.add)
 
-        def add_bias_and_residual_on_tensor(i):
-            for half in range(HALVES):
-                cols = slice(BANK * half, BANK * (half + 1))
-                both = psum_sum.tile([P, BANK], F32)
-                nc.tensor.matmul(both[:], lhsT=identity_bf[:], rhs=bo_sb[:, i, cols], start=True, stop=False)
-                nc.tensor.matmul(both[:], lhsT=identity_bf[:], rhs=x_sb[:, i, cols], start=False, stop=True)
-                nc.scalar.copy(out=o_sb[:, i, cols], in_=both[:])
-
         def add_product(i):
             for half in range(HALVES):
                 cols = slice(BANK * half, BANK * (half + 1))
@@ -185,17 +181,30 @@ def tile_multiheadattn_pb_kernel(tc, h_attn, Wo_words, Wo_scales, bo, x, gamma, 
                     accum_out=o_sums[:, column : column + 1],
                 )
 
-        def average(row_sums, result):
+        def average(row_sums, result, scale, bias):
             columns = row_sums.shape[1]
             summed = psum_stat.tile([P, TILES_PER_BATCH * HALVES], F32)
             nc.tensor.matmul(summed[:, :columns], lhsT=averager[:], rhs=row_sums, start=True, stop=True)
-            nc.scalar.activation(
-                out=spread[:, :columns], in_=summed[:, :columns], func=FUNC.Identity, accum_out=result
-            )
+            if bias is None:
+                nc.scalar.activation(
+                    out=spread[:, :columns], in_=summed[:, :columns], func=FUNC.Identity, scale=scale, accum_out=result
+                )
+            else:
+                nc.scalar.activation(
+                    out=spread[:, :columns], in_=summed[:, :columns], func=FUNC.Identity, scale=scale, bias=bias,
+                    accum_out=result,
+                )
 
-        def take_mean(b):
+        def take_shift(b):
+            first = TILES_PER_BATCH * HALVES * b
+            average(o_sums[:, first : first + HALVES], shift[:, b : b + 1], float(TILES_PER_BATCH), None)
+
+        def take_negmean(b):
             per_batch = TILES_PER_BATCH * HALVES
-            average(o_sums[:, per_batch * b : per_batch * (b + 1)], mean[:, b : b + 1])
+            average(o_sums[:, per_batch * b : per_batch * (b + 1)], negmean[:, b : b + 1], -1.0, None)
+            nc.scalar.activation(
+                out=dsq[:, b : b + 1], in_=negmean[:, b : b + 1], func=FUNC.Square, bias=shift[:, b : b + 1]
+            )
 
         def sum_squares(i):
             b = i // TILES_PER_BATCH
@@ -204,14 +213,25 @@ def tile_multiheadattn_pb_kernel(tc, h_attn, Wo_words, Wo_scales, bo, x, gamma, 
                 in_=o_sb[:, i, :],
                 func=FUNC.Square,
                 scale=-1.0,
-                bias=mean[:, b : b + 1],
+                bias=shift[:, b : b + 1],
                 accum_out=sq_sums[:, i : i + 1],
             )
 
         def take_rstd(b):
-            average(sq_sums[:, TILES_PER_BATCH * b : TILES_PER_BATCH * (b + 1)], var[:, b : b + 1])
+            average(
+                sq_sums[:, TILES_PER_BATCH * b : TILES_PER_BATCH * (b + 1)], e2eps[:, b : b + 1], 1.0, eps_quarter[:]
+            )
             nc.scalar.activation(
-                out=rstd[:, b : b + 1], in_=var[:, b : b + 1], func=FUNC.Abs_reciprocal_sqrt, bias=eps[:]
+                out=rstd[:, b : b + 1],
+                in_=dsq[:, b : b + 1],
+                func=FUNC.Abs_reciprocal_sqrt,
+                scale=-1.0,
+                bias=e2eps[:, b : b + 1],
+            )
+
+        def take_nmr(b):
+            nc.scalar.activation(
+                out=nmr[:, b : b + 1], in_=negmean[:, b : b + 1], func=FUNC.Identity, scale=rstd[:, b : b + 1]
             )
 
         def centre_and_gain(i):
@@ -219,11 +239,14 @@ def tile_multiheadattn_pb_kernel(tc, h_attn, Wo_words, Wo_scales, bo, x, gamma, 
             nc.vector.scalar_tensor_tensor(
                 out=y_sb[:, i, :],
                 in0=o_sb[:, i, :],
-                scalar=mean[:, b : b + 1],
+                scalar=negmean[:, b : b + 1],
                 in1=gamma_sb[:, i % TILES_PER_BATCH, :],
-                op0=ALU.subtract,
+                op0=ALU.add,
                 op1=ALU.mult,
             )
+
+        def store(i):
+            nc.sync.dma_start(out=of_tile(out_view, i), in_=y_sb[:, i, :])
 
         def scale_shift_and_store(i):
             b = i // TILES_PER_BATCH
@@ -235,34 +258,76 @@ def tile_multiheadattn_pb_kernel(tc, h_attn, Wo_words, Wo_scales, bo, x, gamma, 
                 op0=ALU.mult,
                 op1=ALU.add,
             )
-            nc.sync.dma_start(out=of_tile(out_view, i), in_=y_sb[:, i, :])
+            store(i)
+
+        def normalise_on_scalar(i):
+            b = i // TILES_PER_BATCH
+            nc.scalar.activation(
+                out=y_sb[:, i, :],
+                in_=o_sb[:, i, :],
+                func=FUNC.Identity,
+                scale=rstd[:, b : b + 1],
+                bias=nmr[:, b : b + 1],
+            )
+
+        def gain_shift_and_store_on_gpsimd(i):
+            nc.gpsimd.tensor_tensor(
+                out=o_sb[:, i, :], in0=y_sb[:, i, :], in1=gamma_sb[:, i % TILES_PER_BATCH, :], op=ALU.mult
+            )
+            nc.gpsimd.tensor_tensor(
+                out=y_sb[:, i, :], in0=o_sb[:, i, :], in1=beta_sb[:, i % TILES_PER_BATCH, :], op=ALU.add
+            )
+            store(i)
+
+        def add_bias_and_residual_on_gpsimd(i):
+            nc.gpsimd.tensor_tensor(out=o_sb[:, i, :], in0=bo_sb[:, i, :], in1=x_sb[:, i, :], op=ALU.add)
 
         transpose_and_regroup(0)
         transpose_and_regroup(1)
         quantise(0)
         project(0)
-        for step in range(TILES + FINISH_LAG):
-            centred = step - CENTRE_LAG
-            finished = step - FINISH_LAG
-            if 0 <= centred < TILES:
-                sum_squares(centred)
-                if last_of_batch(centred):
-                    take_rstd(centred // TILES_PER_BATCH)
-            if step < TILES:
-                if not summed_by_tensor(step):
-                    add_bias_and_residual(step)
-                if step + 1 < TILES:
-                    quantise(step + 1)
-                if step + 2 < TILES:
-                    transpose_and_regroup(step + 2)
-                if step + 1 < TILES:
-                    if summed_by_tensor(step + 1):
-                        add_bias_and_residual_on_tensor(step + 1)
-                    project(step + 1)
-                add_product(step)
-                if last_of_batch(step):
-                    take_mean(step // TILES_PER_BATCH)
-            if 0 <= finished < TILES:
-                scale_shift_and_store(finished)
-            if 0 <= centred < TILES:
-                centre_and_gain(centred)
+        for i in GPSIMD_SUMMED:
+            add_bias_and_residual_on_gpsimd(i)
+        for step in range(TILES):
+            b = step // TILES_PER_BATCH
+            if step not in GPSIMD_SUMMED:
+                add_bias_and_residual(step)
+            if step + 1 < TILES:
+                quantise(step + 1)
+            if step + 2 < TILES and step <= 3:
+                transpose_and_regroup(step + 2)
+            if step + 1 < TILES:
+                project(step + 1)
+            if step == 3:
+                transpose_and_regroup(6)
+                transpose_and_regroup(7)
+            add_product(step)
+            if first_of_batch(step):
+                take_shift(b)
+            if last_of_batch(step):
+                take_negmean(b)
+            sum_squares(step)
+            if last_of_batch(step):
+                take_rstd(b)
+            if step == 3:
+                take_nmr(0)
+                normalise_on_scalar(2)
+            if step == 4:
+                centre_and_gain(0)
+                normalise_on_scalar(3)
+            if step == 5:
+                centre_and_gain(1)
+            if step == 6:
+                scale_shift_and_store(0)
+            if step == 7:
+                scale_shift_and_store(1)
+        gain_shift_and_store_on_gpsimd(2)
+        centre_and_gain(4)
+        centre_and_gain(5)
+        scale_shift_and_store(4)
+        gain_shift_and_store_on_gpsimd(3)
+        centre_and_gain(6)
+        scale_shift_and_store(5)
+        centre_and_gain(7)
+        scale_shift_and_store(6)
+        scale_shift_and_store(7)

@@ -61,8 +61,7 @@ def tile_multiheadattn_pb_kernel(tc, h_attn, Wo_words, Wo_scales, bo, x, gamma, 
 
     with (
         tc.tile_pool(name="keep", bufs=1) as keep,
-        tc.psum_pool(name="psum_flip", bufs=2) as psum_flip,
-        tc.psum_pool(name="psum_acc", bufs=4) as psum_acc,
+        tc.psum_pool(name="banks", bufs=7) as banks,
         tc.psum_pool(name="psum_stat", bufs=1) as psum_stat,
         tc.manual_schedule(),
     ):
@@ -80,6 +79,7 @@ def tile_multiheadattn_pb_kernel(tc, h_attn, Wo_words, Wo_scales, bo, x, gamma, 
         y_sb = keep.tile([P, TILES, N], F32)
         unread = keep.tile([P, N], BF16)
         identity = keep.tile([P, P], F32)
+        identity_bf = keep.tile([P, P], BF16)
         averager = keep.tile([P, P], F32)
         eps_quarter = keep.tile([P, 1], F32)
         table_warmer = keep.tile([P, 1], F32)
@@ -97,6 +97,7 @@ def tile_multiheadattn_pb_kernel(tc, h_attn, Wo_words, Wo_scales, bo, x, gamma, 
         nc.vector.memset(eps_quarter[:], LN_EPS / TILES_PER_BATCH)
         nc.vector.memset(averager[:], 1.0 / (SEQ * N))
         make_identity(nc, identity[:])
+        make_identity(nc, identity_bf[:])
         nc.scalar.activation(out=table_warmer[:], in_=eps_quarter[:], func=FUNC.Abs_reciprocal_sqrt)
 
         def load_h(i):
@@ -131,7 +132,7 @@ def tile_multiheadattn_pb_kernel(tc, h_attn, Wo_words, Wo_scales, bo, x, gamma, 
 
         def transpose_and_regroup(i):
             h_f32 = h_sb[:, i, :].bitcast(F32)
-            flipped = psum_flip.tile([P, PASSES, PAIRS, P], F32)
+            flipped = banks.tile([P, PASSES, PAIRS, P], F32, tag="bank")
             for g in range(PASSES):
                 for u in range(PAIRS):
                     first = g * WORDS_PER_PASS + u
@@ -151,7 +152,7 @@ def tile_multiheadattn_pb_kernel(tc, h_attn, Wo_words, Wo_scales, bo, x, gamma, 
 
         def project(i):
             for half in range(HALVES):
-                acc = psum_acc.tile([P, BANK], F32)
+                acc = banks.tile([P, BANK], F32, tag="bank")
                 for g in range(PASSES):
                     nc.tensor.matmul_mx(
                         out=acc[:],
@@ -234,13 +235,27 @@ def tile_multiheadattn_pb_kernel(tc, h_attn, Wo_words, Wo_scales, bo, x, gamma, 
                 out=nmr[:, b : b + 1], in_=negmean[:, b : b + 1], func=FUNC.Identity, scale=rstd[:, b : b + 1]
             )
 
+        in_psum = {}
+
+        def lay_in_psum(which, source, t):
+            resident = banks.tile([P, N], BF16, tag="bank")
+            for half in range(HALVES):
+                cols = slice(BANK * half, BANK * (half + 1))
+                nc.tensor.matmul(resident[:, cols], lhsT=identity_bf[:], rhs=source[:, t, cols], start=True, stop=True)
+            in_psum[which, t] = resident
+
+        def operand(which, source, t):
+            if (which, t) in in_psum:
+                return in_psum[which, t][:]
+            return source[:, t, :]
+
         def centre_and_gain(i):
             b = i // TILES_PER_BATCH
             nc.vector.scalar_tensor_tensor(
                 out=y_sb[:, i, :],
                 in0=o_sb[:, i, :],
                 scalar=negmean[:, b : b + 1],
-                in1=gamma_sb[:, i % TILES_PER_BATCH, :],
+                in1=operand("gamma", gamma_sb, i % TILES_PER_BATCH),
                 op0=ALU.add,
                 op1=ALU.mult,
             )
@@ -254,7 +269,7 @@ def tile_multiheadattn_pb_kernel(tc, h_attn, Wo_words, Wo_scales, bo, x, gamma, 
                 out=y_sb[:, i, :],
                 in0=y_sb[:, i, :],
                 scalar=rstd[:, b : b + 1],
-                in1=beta_sb[:, i % TILES_PER_BATCH, :],
+                in1=operand("beta", beta_sb, i % TILES_PER_BATCH),
                 op0=ALU.mult,
                 op1=ALU.add,
             )
@@ -301,6 +316,14 @@ def tile_multiheadattn_pb_kernel(tc, h_attn, Wo_words, Wo_scales, bo, x, gamma, 
             if step == 3:
                 transpose_and_regroup(6)
                 transpose_and_regroup(7)
+            if step == 4:
+                lay_in_psum("gamma", gamma_sb, 0)
+                lay_in_psum("gamma", gamma_sb, 1)
+            if step == 6:
+                lay_in_psum("beta", beta_sb, 0)
+                lay_in_psum("beta", beta_sb, 1)
+                lay_in_psum("gamma", gamma_sb, 2)
+                lay_in_psum("gamma", gamma_sb, 3)
             add_product(step)
             if first_of_batch(step):
                 take_shift(b)

@@ -35,7 +35,7 @@ GAMMA_AFTER = 5
 BETA_AFTER = 7
 
 G_TILES = (2, 3)
-GPSIMD_SUMMED = (3, 4, 5, 6, 7)
+GPSIMD_SUMMED = (5, 6, 7)
 
 FLOPS = 2 * BATCH * SEQ * K * N
 
@@ -61,8 +61,8 @@ def tile_multiheadattn_pb_kernel(tc, h_attn, Wo_words, Wo_scales, bo, x, gamma, 
 
     with (
         tc.tile_pool(name="keep", bufs=1) as keep,
-        tc.psum_pool(name="banks", bufs=7) as banks,
-        tc.psum_pool(name="psum_stat", bufs=1) as psum_stat,
+        tc.tile_pool(name="reused", bufs=1) as reused,
+        tc.psum_pool(name="banks", bufs=8) as banks,
         tc.manual_schedule(),
     ):
         h_sb = keep.tile([P, TILES, K], BF16)
@@ -72,7 +72,7 @@ def tile_multiheadattn_pb_kernel(tc, h_attn, Wo_words, Wo_scales, bo, x, gamma, 
         beta_sb = keep.tile([P, TILES_PER_BATCH, N], BF16)
         w_words = keep.tile([P, PASSES, 2 * N], U8, align_bytes=64)
         w_scales = keep.tile([P, PASSES, N], U8, align_bytes=64)
-        grouped = keep.tile([P, TILES, PASSES, P, PACK], BF16, align_bytes=64)
+        grouped = reused.tile([P, TILES, PASSES, P, PACK], BF16, align_bytes=64, offset=0)
         h_codes = keep.tile([P, TILES, PASSES, P], U32, align_bytes=64)
         h_scales = keep.tile([P, TILES, PASSES, P], U8, align_bytes=64)
         o_sb = keep.tile([P, TILES, N], F32)
@@ -119,16 +119,24 @@ def tile_multiheadattn_pb_kernel(tc, h_attn, Wo_words, Wo_scales, bo, x, gamma, 
         scale_rows = Wo_scales.bitcast(I32).rearrange("g (q r) c -> r q g c", r=4)
         for r in range(4):
             nc.sync.dma_start(out=w_scales[r:P:32, :, :].bitcast(I32), in_=scale_rows[r])
-        for i in range(TILES):
-            if i + 1 < TILES:
-                load_h(i + 1)
-            if i == GAMMA_AFTER + 1:
-                nc.sync.dma_start(out=gamma_sb[:], in_=gamma_view)
-            load_bias_and_residual(i)
-            if i == 0:
-                load_w_words(1)
-            if i == BETA_AFTER:
-                nc.sync.dma_start(out=beta_sb[:], in_=beta_view)
+        load_h(1)
+        load_bias_and_residual(0)
+        load_w_words(1)
+        load_h(2)
+        load_bias_and_residual(1)
+        load_h(3)
+        load_bias_and_residual(2)
+        load_h(4)
+        load_h(5)
+        load_bias_and_residual(3)
+        load_h(6)
+        load_h(7)
+        load_bias_and_residual(4)
+        load_bias_and_residual(5)
+        nc.sync.dma_start(out=gamma_sb[:], in_=gamma_view)
+        load_bias_and_residual(6)
+        load_bias_and_residual(7)
+        nc.sync.dma_start(out=beta_sb[:], in_=beta_view)
 
         def transpose_and_regroup(i):
             h_f32 = h_sb[:, i, :].bitcast(F32)
@@ -149,6 +157,7 @@ def tile_multiheadattn_pb_kernel(tc, h_attn, Wo_words, Wo_scales, bo, x, gamma, 
             )
 
         product = {}
+        summed_at = {}
 
         def project(i):
             for half in range(HALVES):
@@ -176,7 +185,7 @@ def tile_multiheadattn_pb_kernel(tc, h_attn, Wo_words, Wo_scales, bo, x, gamma, 
                     out=o_sb[:, i, cols],
                     in0=product[i, half][:],
                     scalar=1.0,
-                    in1=o_sb[:, i, cols],
+                    in1=summed_at.get(i, o_sb[:, i, :])[:, cols],
                     op0=ALU.mult,
                     op1=ALU.add,
                     accum_out=o_sums[:, column : column + 1],
@@ -184,7 +193,7 @@ def tile_multiheadattn_pb_kernel(tc, h_attn, Wo_words, Wo_scales, bo, x, gamma, 
 
         def average(row_sums, result, scale, bias):
             columns = row_sums.shape[1]
-            summed = psum_stat.tile([P, TILES_PER_BATCH * HALVES], F32)
+            summed = banks.tile([P, TILES_PER_BATCH * HALVES], F32, tag="bank")
             nc.tensor.matmul(summed[:, :columns], lhsT=averager[:], rhs=row_sums, start=True, stop=True)
             if bias is None:
                 nc.scalar.activation(
@@ -294,56 +303,87 @@ def tile_multiheadattn_pb_kernel(tc, h_attn, Wo_words, Wo_scales, bo, x, gamma, 
             )
             store(i)
 
-        def add_bias_and_residual_on_gpsimd(i):
-            nc.gpsimd.tensor_tensor(out=o_sb[:, i, :], in0=bo_sb[:, i, :], in1=x_sb[:, i, :], op=ALU.add)
+        def add_bias_and_residual_on_gpsimd(i, where):
+            nc.gpsimd.tensor_tensor(out=where, in0=bo_sb[:, i, :], in1=x_sb[:, i, :], op=ALU.add)
 
         transpose_and_regroup(0)
         transpose_and_regroup(1)
         quantise(0)
         project(0)
-        for i in GPSIMD_SUMMED:
-            add_bias_and_residual_on_gpsimd(i)
-        for step in range(TILES):
-            b = step // TILES_PER_BATCH
-            if step not in GPSIMD_SUMMED:
-                add_bias_and_residual(step)
-            if step + 1 < TILES:
-                quantise(step + 1)
-            if step + 2 < TILES and step <= 3:
-                transpose_and_regroup(step + 2)
-            if step + 1 < TILES:
-                project(step + 1)
-            if step == 3:
-                transpose_and_regroup(6)
-                transpose_and_regroup(7)
-            if step == 4:
-                lay_in_psum("gamma", gamma_sb, 0)
-                lay_in_psum("gamma", gamma_sb, 1)
-            if step == 6:
-                lay_in_psum("beta", beta_sb, 0)
-                lay_in_psum("beta", beta_sb, 1)
-                lay_in_psum("gamma", gamma_sb, 2)
-                lay_in_psum("gamma", gamma_sb, 3)
-            add_product(step)
-            if first_of_batch(step):
-                take_shift(b)
-            if last_of_batch(step):
-                take_negmean(b)
-            sum_squares(step)
-            if last_of_batch(step):
-                take_rstd(b)
-            if step == 3:
-                take_nmr(0)
-                normalise_on_scalar(2)
-            if step == 4:
-                centre_and_gain(0)
-                normalise_on_scalar(3)
-            if step == 5:
-                centre_and_gain(1)
-            if step == 6:
-                scale_shift_and_store(0)
-            if step == 7:
-                scale_shift_and_store(1)
+
+        add_bias_and_residual(0)
+        quantise(1)
+        transpose_and_regroup(2)
+        project(1)
+        add_product(0)
+        take_shift(0)
+        sum_squares(0)
+
+        add_bias_and_residual(1)
+        quantise(2)
+        transpose_and_regroup(3)
+        project(2)
+        transpose_and_regroup(4)
+        add_product(1)
+        sum_squares(1)
+
+        add_bias_and_residual(2)
+        quantise(3)
+        quantise(4)
+        transpose_and_regroup(5)
+        project(3)
+        transpose_and_regroup(6)
+        add_product(2)
+        sum_squares(2)
+
+        add_bias_and_residual(3)
+        quantise(5)
+        quantise(6)
+        transpose_and_regroup(7)
+        project(4)
+        add_product(3)
+        take_negmean(0)
+        sum_squares(3)
+        take_rstd(0)
+        take_nmr(0)
+        normalise_on_scalar(2)
+
+        add_bias_and_residual(4)
+        quantise(7)
+        first_sum = reused.tile([P, N], F32, offset=0)
+        summed_at[5] = first_sum
+        add_bias_and_residual_on_gpsimd(5, first_sum[:])
+        add_bias_and_residual_on_gpsimd(6, o_sb[:, 6, :])
+        add_bias_and_residual_on_gpsimd(7, o_sb[:, 7, :])
+        project(5)
+        lay_in_psum("gamma", gamma_sb, 0)
+        lay_in_psum("gamma", gamma_sb, 1)
+        add_product(4)
+        take_shift(1)
+        sum_squares(4)
+        centre_and_gain(0)
+        normalise_on_scalar(3)
+
+        project(6)
+        add_product(5)
+        sum_squares(5)
+        centre_and_gain(1)
+
+        project(7)
+        lay_in_psum("beta", beta_sb, 0)
+        lay_in_psum("beta", beta_sb, 1)
+        lay_in_psum("gamma", gamma_sb, 2)
+        lay_in_psum("gamma", gamma_sb, 3)
+        add_product(6)
+        sum_squares(6)
+        scale_shift_and_store(0)
+
+        add_product(7)
+        take_negmean(1)
+        sum_squares(7)
+        take_rstd(1)
+        scale_shift_and_store(1)
+
         gain_shift_and_store_on_gpsimd(2)
         centre_and_gain(4)
         centre_and_gain(5)

@@ -301,7 +301,7 @@ def tile_multiheadattn_pb_kernel(tc, h_attn, Wo_words, Wo_scales, bo, x, gamma, 
             nc.gpsimd.tensor_tensor(
                 out=y_sb[:, i, :], in0=o_sb[:, i, :], in1=beta_sb[:, i % TILES_PER_BATCH, :], op=ALU.add
             )
-            store(i)
+            nc.scalar.dma_start(out=of_tile(out_view, i), in_=y_sb[:, i, :])
 
         def add_bias_and_residual_on_gpsimd(i, where):
             nc.gpsimd.tensor_tensor(out=where, in0=bo_sb[:, i, :], in1=x_sb[:, i, :], op=ALU.add)
@@ -333,20 +333,12 @@ def tile_multiheadattn_pb_kernel(tc, h_attn, Wo_words, Wo_scales, bo, x, gamma, 
         transpose_and_regroup(5)
         project(3)
         transpose_and_regroup(6)
-        add_product(2)
-        sum_squares(2)
 
         add_bias_and_residual(3)
         quantise(5)
         quantise(6)
         transpose_and_regroup(7)
         project(4)
-        add_product(3)
-        take_negmean(0)
-        sum_squares(3)
-        take_rstd(0)
-        take_nmr(0)
-        normalise_on_scalar(2)
 
         add_bias_and_residual(4)
         quantise(7)
@@ -355,42 +347,47 @@ def tile_multiheadattn_pb_kernel(tc, h_attn, Wo_words, Wo_scales, bo, x, gamma, 
         add_bias_and_residual_on_gpsimd(5, first_sum[:])
         add_bias_and_residual_on_gpsimd(6, o_sb[:, 6, :])
         add_bias_and_residual_on_gpsimd(7, o_sb[:, 7, :])
+
         project(5)
+        add_product(2)
+        sum_squares(2)
+        project(6)
+        add_product(3)
+        take_negmean(0)
+        sum_squares(3)
+        take_rstd(0)
+        take_nmr(0)
+        normalise_on_scalar(2)
         lay_in_psum("gamma", gamma_sb, 0)
         lay_in_psum("gamma", gamma_sb, 1)
         add_product(4)
         take_shift(1)
         sum_squares(4)
-        centre_and_gain(0)
         normalise_on_scalar(3)
-
-        project(6)
+        project(7)
         add_product(5)
         sum_squares(5)
-        centre_and_gain(1)
-
-        project(7)
+        centre_and_gain(0)
         lay_in_psum("beta", beta_sb, 0)
         lay_in_psum("beta", beta_sb, 1)
-        lay_in_psum("gamma", gamma_sb, 2)
-        lay_in_psum("gamma", gamma_sb, 3)
         add_product(6)
         sum_squares(6)
-        scale_shift_and_store(0)
-
+        centre_and_gain(1)
+        lay_in_psum("gamma", gamma_sb, 2)
+        lay_in_psum("gamma", gamma_sb, 3)
         add_product(7)
         take_negmean(1)
         sum_squares(7)
         take_rstd(1)
+        scale_shift_and_store(0)
         scale_shift_and_store(1)
-
         gain_shift_and_store_on_gpsimd(2)
+        gain_shift_and_store_on_gpsimd(3)
         centre_and_gain(4)
         centre_and_gain(5)
-        scale_shift_and_store(4)
-        gain_shift_and_store_on_gpsimd(3)
         centre_and_gain(6)
-        scale_shift_and_store(5)
         centre_and_gain(7)
+        scale_shift_and_store(4)
+        scale_shift_and_store(5)
         scale_shift_and_store(6)
         scale_shift_and_store(7)

@@ -34,8 +34,8 @@ TENSOR_SUMMED = 0
 GAMMA_AFTER = 5
 BETA_AFTER = 7
 
-G_TILES = (2, 3)
-GPSIMD_SUMMED = (5, 6, 7)
+G_TILES = (3, 7)
+GPSIMD_SUMMED = (4, 5, 6, 7)
 
 FLOPS = 2 * BATCH * SEQ * K * N
 
@@ -253,6 +253,23 @@ def tile_multiheadattn_pb_kernel(tc, h_attn, Wo_words, Wo_scales, bo, x, gamma, 
                 nc.tensor.matmul(resident[:, cols], lhsT=identity_bf[:], rhs=source[:, t, cols], start=True, stop=True)
             in_psum[which, t] = resident
 
+        turned_round = {}
+
+        def turn_round(which, source, t):
+            words = source[:, t, :].bitcast(F32)
+            flipped = banks.tile([P, BANK // P, P], F32, tag="bank")
+            for c in range(BANK // P):
+                nc.tensor.transpose(flipped[:, c, :], words[:, P * c : P * (c + 1)], identity[:])
+            turned = keep.tile([P, BANK // P, P], F32)
+            nc.scalar.copy(out=turned[:], in_=flipped[:])
+            turned_round[which, t] = turned
+
+        def turn_back_into_psum(which, t):
+            back = banks.tile([P, BANK], F32, tag="bank")
+            for c in range(BANK // P):
+                nc.tensor.transpose(back[:, P * c : P * (c + 1)], turned_round[which, t][:, c, :], identity[:])
+            in_psum[which, t] = back[:].bitcast(BF16)
+
         def operand(which, source, t):
             if (which, t) in in_psum:
                 return in_psum[which, t][:]
@@ -293,6 +310,16 @@ def tile_multiheadattn_pb_kernel(tc, h_attn, Wo_words, Wo_scales, bo, x, gamma, 
                 scale=rstd[:, b : b + 1],
                 bias=nmr[:, b : b + 1],
             )
+
+        def scale_on_scalar(i):
+            b = i // TILES_PER_BATCH
+            nc.scalar.activation(out=o_sb[:, i, :], in_=y_sb[:, i, :], func=FUNC.Identity, scale=rstd[:, b : b + 1])
+
+        def shift_and_store_on_gpsimd(i):
+            nc.gpsimd.tensor_tensor(
+                out=y_sb[:, i, :], in0=o_sb[:, i, :], in1=beta_sb[:, i % TILES_PER_BATCH, :], op=ALU.add
+            )
+            nc.scalar.dma_start(out=of_tile(out_view, i), in_=y_sb[:, i, :])
 
         def gain_shift_and_store_on_gpsimd(i):
             nc.gpsimd.tensor_tensor(
@@ -340,54 +367,56 @@ def tile_multiheadattn_pb_kernel(tc, h_attn, Wo_words, Wo_scales, bo, x, gamma, 
         transpose_and_regroup(7)
         project(4)
 
-        add_bias_and_residual(4)
         quantise(7)
         first_sum = reused.tile([P, N], F32, offset=0)
-        summed_at[5] = first_sum
-        add_bias_and_residual_on_gpsimd(5, first_sum[:])
+        summed_at[4] = first_sum
+        add_bias_and_residual_on_gpsimd(4, first_sum[:])
+        add_bias_and_residual_on_gpsimd(5, o_sb[:, 5, :])
         add_bias_and_residual_on_gpsimd(6, o_sb[:, 6, :])
         add_bias_and_residual_on_gpsimd(7, o_sb[:, 7, :])
 
         project(5)
         add_product(2)
         sum_squares(2)
-        project(6)
+        lay_in_psum("gamma", gamma_sb, 0)
+        lay_in_psum("gamma", gamma_sb, 1)
         add_product(3)
         take_negmean(0)
         sum_squares(3)
         take_rstd(0)
         take_nmr(0)
-        normalise_on_scalar(2)
-        lay_in_psum("gamma", gamma_sb, 0)
-        lay_in_psum("gamma", gamma_sb, 1)
+        normalise_on_scalar(3)
+        lay_in_psum("gamma", gamma_sb, 2)
         add_product(4)
         take_shift(1)
         sum_squares(4)
-        normalise_on_scalar(3)
-        project(7)
+        project(6)
+        centre_and_gain(0)
         add_product(5)
         sum_squares(5)
-        centre_and_gain(0)
-        lay_in_psum("beta", beta_sb, 0)
-        lay_in_psum("beta", beta_sb, 1)
+        project(7)
+        centre_and_gain(1)
         add_product(6)
         sum_squares(6)
-        centre_and_gain(1)
-        lay_in_psum("gamma", gamma_sb, 2)
-        lay_in_psum("gamma", gamma_sb, 3)
+        lay_in_psum("beta", beta_sb, 0)
+        lay_in_psum("beta", beta_sb, 1)
+        centre_and_gain(2)
+        scale_on_scalar(2)
         add_product(7)
         take_negmean(1)
         sum_squares(7)
         take_rstd(1)
+        take_nmr(1)
+        normalise_on_scalar(7)
+        lay_in_psum("beta", beta_sb, 2)
         scale_shift_and_store(0)
         scale_shift_and_store(1)
-        gain_shift_and_store_on_gpsimd(2)
         gain_shift_and_store_on_gpsimd(3)
+        shift_and_store_on_gpsimd(2)
+        gain_shift_and_store_on_gpsimd(7)
         centre_and_gain(4)
         centre_and_gain(5)
         centre_and_gain(6)
-        centre_and_gain(7)
         scale_shift_and_store(4)
         scale_shift_and_store(5)
         scale_shift_and_store(6)
-        scale_shift_and_store(7)

@@ -35,7 +35,12 @@ GAMMA_AFTER = 5
 BETA_AFTER = 7
 
 G_TILES = (3, 7)
+SQUARE_SUMS = TILES_PER_BATCH + 1
 GPSIMD_SUMMED = (4, 5, 6, 7)
+
+WHOLE = slice(0, N)
+FIRST_HALF = slice(0, BANK)
+SECOND_HALF = slice(BANK, N)
 
 FLOPS = 2 * BATCH * SEQ * K * N
 
@@ -81,10 +86,10 @@ def tile_multiheadattn_pb_kernel(tc, h_attn, Wo_words, Wo_scales, bo, x, gamma, 
         identity = keep.tile([P, P], F32)
         identity_bf = keep.tile([P, P], BF16)
         averager = keep.tile([P, P], F32)
-        eps_quarter = keep.tile([P, 1], F32)
+        eps_part = keep.tile([P, 1], F32)
         table_warmer = keep.tile([P, 1], F32)
         o_sums = keep.tile([P, TILES * HALVES], F32)
-        sq_sums = keep.tile([P, TILES], F32)
+        sq_sums = keep.tile([P, BATCH, SQUARE_SUMS], F32)
         spread = keep.tile([P, TILES_PER_BATCH * HALVES], F32)
         shift = keep.tile([P, BATCH], F32)
         negmean = keep.tile([P, BATCH], F32)
@@ -94,11 +99,11 @@ def tile_multiheadattn_pb_kernel(tc, h_attn, Wo_words, Wo_scales, bo, x, gamma, 
         nmr = keep.tile([P, BATCH], F32)
 
         nc.vector.memset(w_scales[:].bitcast(I32), 0)
-        nc.vector.memset(eps_quarter[:], LN_EPS / TILES_PER_BATCH)
+        nc.vector.memset(eps_part[:], LN_EPS / SQUARE_SUMS)
         nc.vector.memset(averager[:], 1.0 / (SEQ * N))
         make_identity(nc, identity[:])
         make_identity(nc, identity_bf[:])
-        nc.scalar.activation(out=table_warmer[:], in_=eps_quarter[:], func=FUNC.Abs_reciprocal_sqrt)
+        nc.scalar.activation(out=table_warmer[:], in_=eps_part[:], func=FUNC.Abs_reciprocal_sqrt)
 
         def load_h(i):
             nc.sync.dma_start(out=h_sb[:, i, :], in_=of_tile(h_view, i))
@@ -138,7 +143,9 @@ def tile_multiheadattn_pb_kernel(tc, h_attn, Wo_words, Wo_scales, bo, x, gamma, 
         load_bias_and_residual(7)
         nc.sync.dma_start(out=beta_sb[:], in_=beta_view)
 
-        def transpose_and_regroup(i):
+        flipped_of = {}
+
+        def transpose(i):
             h_f32 = h_sb[:, i, :].bitcast(F32)
             flipped = banks.tile([P, PASSES, PAIRS, P], F32, tag="bank")
             for g in range(PASSES):
@@ -147,7 +154,10 @@ def tile_multiheadattn_pb_kernel(tc, h_attn, Wo_words, Wo_scales, bo, x, gamma, 
                     nc.tensor.transpose(
                         flipped[:, g, u, :], h_f32[:, first : (g + 1) * WORDS_PER_PASS : PAIRS], identity[:]
                     )
-            nc.scalar.copy(out=grouped[:, i].bitcast(F32), in_=flipped[:].rearrange("p g u m -> p g m u"))
+            flipped_of[i] = flipped
+
+        def regroup(i):
+            nc.scalar.copy(out=grouped[:, i].bitcast(F32), in_=flipped_of[i][:].rearrange("p g u m -> p g m u"))
 
         def quantise(i):
             nc.vector.quantize_mx(
@@ -218,19 +228,22 @@ def tile_multiheadattn_pb_kernel(tc, h_attn, Wo_words, Wo_scales, bo, x, gamma, 
 
         def sum_squares(i):
             b = i // TILES_PER_BATCH
-            nc.scalar.activation(
-                out=unread[:],
-                in_=o_sb[:, i, :],
-                func=FUNC.Square,
-                scale=-1.0,
-                bias=shift[:, b : b + 1],
-                accum_out=sq_sums[:, i : i + 1],
-            )
+            pieces = HALVES if last_of_batch(i) else 1
+            width = N // pieces
+            for piece in range(pieces):
+                cols = slice(width * piece, width * (piece + 1))
+                column = i % TILES_PER_BATCH + piece
+                nc.scalar.activation(
+                    out=unread[:, cols],
+                    in_=o_sb[:, i, cols],
+                    func=FUNC.Square,
+                    scale=-1.0,
+                    bias=shift[:, b : b + 1],
+                    accum_out=sq_sums[:, b, column : column + 1],
+                )
 
         def take_rstd(b):
-            average(
-                sq_sums[:, TILES_PER_BATCH * b : TILES_PER_BATCH * (b + 1)], e2eps[:, b : b + 1], 1.0, eps_quarter[:]
-            )
+            average(sq_sums[:, b, :], e2eps[:, b : b + 1], 1.0, eps_part[:])
             nc.scalar.activation(
                 out=rstd[:, b : b + 1],
                 in_=dsq[:, b : b + 1],
@@ -253,23 +266,6 @@ def tile_multiheadattn_pb_kernel(tc, h_attn, Wo_words, Wo_scales, bo, x, gamma, 
                 nc.tensor.matmul(resident[:, cols], lhsT=identity_bf[:], rhs=source[:, t, cols], start=True, stop=True)
             in_psum[which, t] = resident
 
-        turned_round = {}
-
-        def turn_round(which, source, t):
-            words = source[:, t, :].bitcast(F32)
-            flipped = banks.tile([P, BANK // P, P], F32, tag="bank")
-            for c in range(BANK // P):
-                nc.tensor.transpose(flipped[:, c, :], words[:, P * c : P * (c + 1)], identity[:])
-            turned = keep.tile([P, BANK // P, P], F32)
-            nc.scalar.copy(out=turned[:], in_=flipped[:])
-            turned_round[which, t] = turned
-
-        def turn_back_into_psum(which, t):
-            back = banks.tile([P, BANK], F32, tag="bank")
-            for c in range(BANK // P):
-                nc.tensor.transpose(back[:, P * c : P * (c + 1)], turned_round[which, t][:, c, :], identity[:])
-            in_psum[which, t] = back[:].bitcast(BF16)
-
         def operand(which, source, t):
             if (which, t) in in_psum:
                 return in_psum[which, t][:]
@@ -286,87 +282,92 @@ def tile_multiheadattn_pb_kernel(tc, h_attn, Wo_words, Wo_scales, bo, x, gamma, 
                 op1=ALU.mult,
             )
 
-        def store(i):
-            nc.sync.dma_start(out=of_tile(out_view, i), in_=y_sb[:, i, :])
+        def store(i, cols):
+            nc.sync.dma_start(out=of_tile(out_view, i)[:, cols], in_=y_sb[:, i, cols])
 
-        def scale_shift_and_store(i):
+        def scale_shift_and_store(i, cols=WHOLE):
             b = i // TILES_PER_BATCH
             nc.vector.scalar_tensor_tensor(
-                out=y_sb[:, i, :],
-                in0=y_sb[:, i, :],
+                out=y_sb[:, i, cols],
+                in0=y_sb[:, i, cols],
                 scalar=rstd[:, b : b + 1],
-                in1=operand("beta", beta_sb, i % TILES_PER_BATCH),
+                in1=operand("beta", beta_sb, i % TILES_PER_BATCH)[:, cols],
                 op0=ALU.mult,
                 op1=ALU.add,
             )
-            store(i)
+            store(i, cols)
 
-        def normalise_on_scalar(i):
+        def normalise_on_scalar(i, cols):
             b = i // TILES_PER_BATCH
             nc.scalar.activation(
-                out=y_sb[:, i, :],
-                in_=o_sb[:, i, :],
+                out=y_sb[:, i, cols],
+                in_=o_sb[:, i, cols],
                 func=FUNC.Identity,
                 scale=rstd[:, b : b + 1],
                 bias=nmr[:, b : b + 1],
             )
 
-        def scale_on_scalar(i):
+        def scale_on_scalar(i, cols):
             b = i // TILES_PER_BATCH
-            nc.scalar.activation(out=o_sb[:, i, :], in_=y_sb[:, i, :], func=FUNC.Identity, scale=rstd[:, b : b + 1])
+            nc.scalar.activation(
+                out=o_sb[:, i, cols], in_=y_sb[:, i, cols], func=FUNC.Identity, scale=rstd[:, b : b + 1]
+            )
 
-        def shift_and_store_on_gpsimd(i):
+        def shift_and_store_on_gpsimd(i, cols):
             nc.gpsimd.tensor_tensor(
-                out=y_sb[:, i, :], in0=o_sb[:, i, :], in1=beta_sb[:, i % TILES_PER_BATCH, :], op=ALU.add
+                out=y_sb[:, i, cols], in0=o_sb[:, i, cols], in1=beta_sb[:, i % TILES_PER_BATCH, cols], op=ALU.add
             )
-            nc.scalar.dma_start(out=of_tile(out_view, i), in_=y_sb[:, i, :])
+            nc.scalar.dma_start(out=of_tile(out_view, i)[:, cols], in_=y_sb[:, i, cols])
 
-        def gain_shift_and_store_on_gpsimd(i):
+        def gain_shift_and_store_on_gpsimd(i, cols):
             nc.gpsimd.tensor_tensor(
-                out=o_sb[:, i, :], in0=y_sb[:, i, :], in1=gamma_sb[:, i % TILES_PER_BATCH, :], op=ALU.mult
+                out=o_sb[:, i, cols], in0=y_sb[:, i, cols], in1=gamma_sb[:, i % TILES_PER_BATCH, cols], op=ALU.mult
             )
             nc.gpsimd.tensor_tensor(
-                out=y_sb[:, i, :], in0=o_sb[:, i, :], in1=beta_sb[:, i % TILES_PER_BATCH, :], op=ALU.add
+                out=y_sb[:, i, cols], in0=o_sb[:, i, cols], in1=beta_sb[:, i % TILES_PER_BATCH, cols], op=ALU.add
             )
-            nc.scalar.dma_start(out=of_tile(out_view, i), in_=y_sb[:, i, :])
+            nc.scalar.dma_start(out=of_tile(out_view, i)[:, cols], in_=y_sb[:, i, cols])
 
         def add_bias_and_residual_on_gpsimd(i, where):
             nc.gpsimd.tensor_tensor(out=where, in0=bo_sb[:, i, :], in1=x_sb[:, i, :], op=ALU.add)
 
-        transpose_and_regroup(0)
-        transpose_and_regroup(1)
+        transpose(0)
+        regroup(0)
+        transpose(1)
+        regroup(1)
         quantise(0)
         project(0)
-
         add_bias_and_residual(0)
         quantise(1)
-        transpose_and_regroup(2)
+        transpose(2)
+        regroup(2)
         project(1)
         add_product(0)
         take_shift(0)
         sum_squares(0)
-
         add_bias_and_residual(1)
         quantise(2)
-        transpose_and_regroup(3)
+        transpose(3)
+        regroup(3)
         project(2)
-        transpose_and_regroup(4)
+        transpose(4)
+        regroup(4)
         add_product(1)
         sum_squares(1)
-
         add_bias_and_residual(2)
         quantise(3)
         quantise(4)
-        transpose_and_regroup(5)
+        transpose(5)
+        regroup(5)
         project(3)
-        transpose_and_regroup(6)
-
+        transpose(6)
+        regroup(6)
         add_bias_and_residual(3)
         quantise(5)
         quantise(6)
-        transpose_and_regroup(7)
+        transpose(7)
+        regroup(7)
         project(4)
-
         quantise(7)
         first_sum = reused.tile([P, N], F32, offset=0)
         summed_at[4] = first_sum
@@ -374,7 +375,6 @@ def tile_multiheadattn_pb_kernel(tc, h_attn, Wo_words, Wo_scales, bo, x, gamma, 
         add_bias_and_residual_on_gpsimd(5, o_sb[:, 5, :])
         add_bias_and_residual_on_gpsimd(6, o_sb[:, 6, :])
         add_bias_and_residual_on_gpsimd(7, o_sb[:, 7, :])
-
         project(5)
         add_product(2)
         sum_squares(2)
@@ -385,7 +385,7 @@ def tile_multiheadattn_pb_kernel(tc, h_attn, Wo_words, Wo_scales, bo, x, gamma, 
         sum_squares(3)
         take_rstd(0)
         take_nmr(0)
-        normalise_on_scalar(3)
+        normalise_on_scalar(3, WHOLE)
         lay_in_psum("gamma", gamma_sb, 2)
         add_product(4)
         take_shift(1)
@@ -400,23 +400,23 @@ def tile_multiheadattn_pb_kernel(tc, h_attn, Wo_words, Wo_scales, bo, x, gamma, 
         sum_squares(6)
         lay_in_psum("beta", beta_sb, 0)
         lay_in_psum("beta", beta_sb, 1)
+        lay_in_psum("beta", beta_sb, 2)
         centre_and_gain(2)
-        scale_on_scalar(2)
         add_product(7)
-        take_negmean(1)
         sum_squares(7)
+        take_negmean(1)
         take_rstd(1)
         take_nmr(1)
-        normalise_on_scalar(7)
-        lay_in_psum("beta", beta_sb, 2)
+        normalise_on_scalar(7, WHOLE)
         scale_shift_and_store(0)
         scale_shift_and_store(1)
-        gain_shift_and_store_on_gpsimd(3)
-        shift_and_store_on_gpsimd(2)
-        gain_shift_and_store_on_gpsimd(7)
+        scale_shift_and_store(2)
+        gain_shift_and_store_on_gpsimd(3, WHOLE)
+        gain_shift_and_store_on_gpsimd(7, WHOLE)
         centre_and_gain(4)
         centre_and_gain(5)
-        centre_and_gain(6)
         scale_shift_and_store(4)
         scale_shift_and_store(5)
-        scale_shift_and_store(6)
+        centre_and_gain(6)
+        scale_shift_and_store(6, FIRST_HALF)
+        scale_shift_and_store(6, SECOND_HALF)

@@ -41,6 +41,9 @@ GPSIMD_SUMMED = (4, 5, 6, 7)
 WHOLE = slice(0, N)
 FIRST_HALF = slice(0, BANK)
 SECOND_HALF = slice(BANK, N)
+SHARE = 640
+VECTOR_SHARE = slice(0, SHARE)
+GPSIMD_SHARE = slice(SHARE, N)
 
 FLOPS = 2 * BATCH * SEQ * K * N
 
@@ -187,8 +190,8 @@ def tile_multiheadattn_pb_kernel(tc, h_attn, Wo_words, Wo_scales, bo, x, gamma, 
         def add_bias_and_residual(i):
             nc.vector.tensor_tensor(out=o_sb[:, i, :], in0=bo_sb[:, i, :], in1=x_sb[:, i, :], op=ALU.add)
 
-        def add_product(i):
-            for half in range(HALVES):
+        def add_product(i, halves=(0, 1)):
+            for half in halves:
                 cols = slice(BANK * half, BANK * (half + 1))
                 column = HALVES * i + half
                 nc.vector.scalar_tensor_tensor(
@@ -328,6 +331,17 @@ def tile_multiheadattn_pb_kernel(tc, h_attn, Wo_words, Wo_scales, bo, x, gamma, 
             )
             nc.scalar.dma_start(out=of_tile(out_view, i)[:, cols], in_=y_sb[:, i, cols])
 
+        def shift_and_store_on_vector(i, cols):
+            nc.vector.tensor_tensor(
+                out=y_sb[:, i, cols], in0=o_sb[:, i, cols], in1=beta_sb[:, i % TILES_PER_BATCH, cols], op=ALU.add
+            )
+            store(i, cols)
+
+        def gain_on_gpsimd(i):
+            nc.gpsimd.tensor_tensor(
+                out=o_sb[:, i, :], in0=y_sb[:, i, :], in1=gamma_sb[:, i % TILES_PER_BATCH, :], op=ALU.mult
+            )
+
         def add_bias_and_residual_on_gpsimd(i, where):
             nc.gpsimd.tensor_tensor(out=where, in0=bo_sb[:, i, :], in1=x_sb[:, i, :], op=ALU.add)
 
@@ -402,6 +416,7 @@ def tile_multiheadattn_pb_kernel(tc, h_attn, Wo_words, Wo_scales, bo, x, gamma, 
         lay_in_psum("beta", beta_sb, 1)
         lay_in_psum("beta", beta_sb, 2)
         centre_and_gain(2)
+        scale_on_scalar(2, GPSIMD_SHARE)
         add_product(7)
         sum_squares(7)
         take_negmean(1)
@@ -410,9 +425,12 @@ def tile_multiheadattn_pb_kernel(tc, h_attn, Wo_words, Wo_scales, bo, x, gamma, 
         normalise_on_scalar(7, WHOLE)
         scale_shift_and_store(0)
         scale_shift_and_store(1)
-        scale_shift_and_store(2)
+        scale_shift_and_store(2, VECTOR_SHARE)
         gain_shift_and_store_on_gpsimd(3, WHOLE)
-        gain_shift_and_store_on_gpsimd(7, WHOLE)
+        shift_and_store_on_gpsimd(2, GPSIMD_SHARE)
+        gain_on_gpsimd(7)
+        shift_and_store_on_gpsimd(7, FIRST_HALF)
+        shift_and_store_on_gpsimd(7, SECOND_HALF)
         centre_and_gain(4)
         centre_and_gain(5)
         scale_shift_and_store(4)

import concourse.mybir as mybir
from concourse.masks import make_identity

F32 = mybir.dt.float32
BF16 = mybir.dt.bfloat16
I32 = mybir.dt.int32
U32 = mybir.dt.uint32
U8 = mybir.dt.uint8
FP8X4 = mybir.dt.float8_e4m3fn_x4
FP4X4 = mybir.dt.float4_e2m1fn_x4
ALU = mybir.AluOpType
FUNC = mybir.ActivationFunctionType

P = 128
BATCH = 2
SEQ = 512
K = 1024
N = 1024
LN_EPS = 1e-5

PACK = 4
K_PASS = P * PACK
PASSES = K // K_PASS
PAIRS = PACK // 2
WORDS_PER_PASS = K_PASS // 2

TILES_PER_BATCH = SEQ // P
TILES = BATCH * TILES_PER_BATCH
BANK = 512
HALVES = N // BANK

TENSOR_SUMMED = 0

GAMMA_AFTER = 5
BETA_AFTER = 7

G_TILES = (3, 7)
SQUARE_SUMS = TILES_PER_BATCH + 1
GPSIMD_SUMMED = (4, 5, 6, 7)

WHOLE = slice(0, N)
FIRST_HALF = slice(0, BANK)
SECOND_HALF = slice(BANK, N)
SHARE = 640
VECTOR_SHARE = slice(0, SHARE)
GPSIMD_SHARE = slice(SHARE, N)

FLOPS = 2 * BATCH * SEQ * K * N


def tile_multiheadattn_pb_kernel(tc, h_attn, Wo_words, Wo_scales, bo, x, gamma, beta, out):
    nc = tc.nc

    h_view = h_attn.rearrange("b (p t) k -> p b t k", t=TILES_PER_BATCH)
    bo_view = bo.rearrange("b (p t) n -> p b t n", t=TILES_PER_BATCH)
    x_view = x.rearrange("b (p t) n -> p b t n", t=TILES_PER_BATCH)
    out_view = out.rearrange("b (p t) n -> p b t n", t=TILES_PER_BATCH)
    gamma_view = gamma.rearrange("(p t) n -> p t n", t=TILES_PER_BATCH)
    beta_view = beta.rearrange("(p t) n -> p t n", t=TILES_PER_BATCH)

    def of_tile(view, i):
        return view[:, i // TILES_PER_BATCH, i % TILES_PER_BATCH, :]

    def first_of_batch(i):
        return i % TILES_PER_BATCH == 0

    def last_of_batch(i):
        return i % TILES_PER_BATCH == TILES_PER_BATCH - 1

    with (
        tc.tile_pool(name="keep", bufs=1) as keep,
        tc.tile_pool(name="reused", bufs=1) as reused,
        tc.psum_pool(name="banks", bufs=8) as banks,
        tc.manual_schedule(),
    ):
        h_sb = keep.tile([P, TILES, K], BF16)
        bo_sb = keep.tile([P, TILES, N], BF16)
        x_sb = keep.tile([P, TILES, N], BF16)
        gamma_sb = keep.tile([P, TILES_PER_BATCH, N], BF16)
        beta_sb = keep.tile([P, TILES_PER_BATCH, N], BF16)
        w_words = keep.tile([P, PASSES, 2 * N], U8, align_bytes=64)
        w_scales = keep.tile([P, PASSES, N], U8, align_bytes=64)
        grouped = reused.tile([P, TILES, PASSES, P, PACK], BF16, align_bytes=64, offset=0)
        h_codes = keep.tile([P, TILES, PASSES, P], U32, align_bytes=64)
        h_scales = keep.tile([P, TILES, PASSES, P], U8, align_bytes=64)
        o_sb = keep.tile([P, TILES, N], F32)
        y_sb = keep.tile([P, TILES, N], F32)
        unread = keep.tile([P, N], BF16)
        identity = keep.tile([P, P], F32)
        identity_bf = keep.tile([P, P], BF16)
        averager = keep.tile([P, P], F32)
        eps_part = keep.tile([P, 1], F32)
        table_warmer = keep.tile([P, 1], F32)
        o_sums = keep.tile([P, TILES * HALVES], F32)
        sq_sums = keep.tile([P, BATCH, SQUARE_SUMS], F32)
        spread = keep.tile([P, TILES_PER_BATCH * HALVES], F32)
        shift = keep.tile([P, BATCH], F32)
        negmean = keep.tile([P, BATCH], F32)
        e2eps = keep.tile([P, BATCH], F32)
        dsq = keep.tile([P, BATCH], F32)
        rstd = keep.tile([P, BATCH], F32)
        nmr = keep.tile([P, BATCH], F32)

        nc.vector.memset(w_scales[:].bitcast(I32), 0)
        nc.vector.memset(eps_part[:], LN_EPS / SQUARE_SUMS)
        nc.vector.memset(averager[:], 1.0 / (SEQ * N))
        make_identity(nc, identity[:])
        make_identity(nc, identity_bf[:])
        nc.scalar.activation(out=table_warmer[:], in_=eps_part[:], func=FUNC.Abs_reciprocal_sqrt)

        def load_h(i):
            nc.sync.dma_start(out=h_sb[:, i, :], in_=of_tile(h_view, i))

        def load_bias_and_residual(i):
            nc.sync.dma_start(out=bo_sb[:, i, :], in_=of_tile(bo_view, i))
            nc.sync.dma_start(out=x_sb[:, i, :], in_=of_tile(x_view, i))

        def load_w_words(half):
            words = slice(BANK // 2 * half, BANK // 2 * (half + 1))
            nc.sync.dma_start(
                out=w_words[:].bitcast(I32)[:, :, words],
                in_=Wo_words.bitcast(I32).rearrange("g p c -> p g c")[:, :, words],
            )

        load_h(0)
        load_w_words(0)
        scale_rows = Wo_scales.bitcast(I32).rearrange("g (q r) c -> r q g c", r=4)
        for r in range(4):
            nc.sync.dma_start(out=w_scales[r:P:32, :, :].bitcast(I32), in_=scale_rows[r])
        load_h(1)
        load_bias_and_residual(0)
        load_w_words(1)
        load_h(2)
        load_bias_and_residual(1)
        load_h(3)
        load_bias_and_residual(2)
        load_h(4)
        load_h(5)
        load_bias_and_residual(3)
        load_h(6)
        load_h(7)
        load_bias_and_residual(4)
        load_bias_and_residual(5)
        nc.sync.dma_start(out=gamma_sb[:], in_=gamma_view)
        load_bias_and_residual(6)
        load_bias_and_residual(7)
        nc.sync.dma_start(out=beta_sb[:], in_=beta_view)

        flipped_of = {}

        def transpose(i):
            h_f32 = h_sb[:, i, :].bitcast(F32)
            flipped = banks.tile([P, PASSES, PAIRS, P], F32, tag="bank")
            for g in range(PASSES):
                for u in range(PAIRS):
                    first = g * WORDS_PER_PASS + u
                    nc.tensor.transpose(
                        flipped[:, g, u, :], h_f32[:, first : (g + 1) * WORDS_PER_PASS : PAIRS], identity[:]
                    )
            flipped_of[i] = flipped

        def regroup(i):
            nc.scalar.copy(out=grouped[:, i].bitcast(F32), in_=flipped_of[i][:].rearrange("p g u m -> p g m u"))

        def quantise(i):
            nc.vector.quantize_mx(
                out=h_codes[:, i].rearrange("p g m -> p (g m)").bitcast(FP8X4),
                scales=h_scales[:, i].rearrange("p g m -> p (g m)"),
                in_=grouped[:, i].rearrange("p g m j -> p (g m j)"),
            )

        product = {}
        summed_at = {}

        def project(i):
            for half in range(HALVES):
                acc = banks.tile([P, BANK], F32, tag="bank")
                for g in range(PASSES):
                    nc.tensor.matmul_mx(
                        out=acc[:],
                        lhsT=h_codes[:, i, g, :].bitcast(FP8X4),
                        lhsT_scale=h_scales[:, i, g, :],
                        rhs=w_words[:, g, 2 * BANK * half : 2 * BANK * (half + 1)].bitcast(FP4X4),
                        rhs_scale=w_scales[:, g, BANK * half : BANK * (half + 1)],
                        start=(g == 0),
                        stop=(g == PASSES - 1),
                    )
                product[i, half] = acc

        def add_bias_and_residual(i):
            nc.vector.tensor_tensor(out=o_sb[:, i, :], in0=bo_sb[:, i, :], in1=x_sb[:, i, :], op=ALU.add)

        def add_product(i, halves=(0, 1)):
            for half in halves:
                cols = slice(BANK * half, BANK * (half + 1))
                column = HALVES * i + half
                nc.vector.scalar_tensor_tensor(
                    out=o_sb[:, i, cols],
                    in0=product[i, half][:],
                    scalar=1.0,
                    in1=summed_at.get(i, o_sb[:, i, :])[:, cols],
                    op0=ALU.mult,
                    op1=ALU.add,
                    accum_out=o_sums[:, column : column + 1],
                )

        def average(row_sums, result, scale, bias):
            columns = row_sums.shape[1]
            summed = banks.tile([P, TILES_PER_BATCH * HALVES], F32, tag="bank")
            nc.tensor.matmul(summed[:, :columns], lhsT=averager[:], rhs=row_sums, start=True, stop=True)
            if bias is None:
                nc.scalar.activation(
                    out=spread[:, :columns], in_=summed[:, :columns], func=FUNC.Identity, scale=scale, accum_out=result
                )
            else:
                nc.scalar.activation(
                    out=spread[:, :columns], in_=summed[:, :columns], func=FUNC.Identity, scale=scale, bias=bias,
                    accum_out=result,
                )

        def take_shift(b):
            first = TILES_PER_BATCH * HALVES * b
            average(o_sums[:, first : first + HALVES], shift[:, b : b + 1], float(TILES_PER_BATCH), None)

        def take_negmean(b):
            per_batch = TILES_PER_BATCH * HALVES
            average(o_sums[:, per_batch * b : per_batch * (b + 1)], negmean[:, b : b + 1], -1.0, None)
            nc.scalar.activation(
                out=dsq[:, b : b + 1], in_=negmean[:, b : b + 1], func=FUNC.Square, bias=shift[:, b : b + 1]
            )

        def sum_squares(i):
            b = i // TILES_PER_BATCH
            pieces = HALVES if last_of_batch(i) else 1
            width = N // pieces
            for piece in range(pieces):
                cols = slice(width * piece, width * (piece + 1))
                column = i % TILES_PER_BATCH + piece
                nc.scalar.activation(
                    out=unread[:, cols],
                    in_=o_sb[:, i, cols],
                    func=FUNC.Square,
                    scale=-1.0,
                    bias=shift[:, b : b + 1],
                    accum_out=sq_sums[:, b, column : column + 1],
                )

        def take_rstd(b):
            average(sq_sums[:, b, :], e2eps[:, b : b + 1], 1.0, eps_part[:])
            nc.scalar.activation(
                out=rstd[:, b : b + 1],
                in_=dsq[:, b : b + 1],
                func=FUNC.Abs_reciprocal_sqrt,
                scale=-1.0,
                bias=e2eps[:, b : b + 1],
            )

        def take_nmr(b):
            nc.scalar.activation(
                out=nmr[:, b : b + 1], in_=negmean[:, b : b + 1], func=FUNC.Identity, scale=rstd[:, b : b + 1]
            )

        in_psum = {}

        def lay_in_psum(which, source, t):
            resident = banks.tile([P, N], BF16, tag="bank")
            for half in range(HALVES):
                cols = slice(BANK * half, BANK * (half + 1))
                nc.tensor.matmul(resident[:, cols], lhsT=identity_bf[:], rhs=source[:, t, cols], start=True, stop=True)
            in_psum[which, t] = resident

        def operand(which, source, t):
            if (which, t) in in_psum:
                return in_psum[which, t][:]
            return source[:, t, :]

        def centre_and_gain(i):
            b = i // TILES_PER_BATCH
            nc.vector.scalar_tensor_tensor(
                out=y_sb[:, i, :],
                in0=o_sb[:, i, :],
                scalar=negmean[:, b : b + 1],
                in1=operand("gamma", gamma_sb, i % TILES_PER_BATCH),
                op0=ALU.add,
                op1=ALU.mult,
            )

        def store(i, cols):
            nc.sync.dma_start(out=of_tile(out_view, i)[:, cols], in_=y_sb[:, i, cols])

        def scale_shift_and_store(i, cols=WHOLE):
            b = i // TILES_PER_BATCH
            nc.vector.scalar_tensor_tensor(
                out=y_sb[:, i, cols],
                in0=y_sb[:, i, cols],
                scalar=rstd[:, b : b + 1],
                in1=operand("beta", beta_sb, i % TILES_PER_BATCH)[:, cols],
                op0=ALU.mult,
                op1=ALU.add,
            )
            store(i, cols)

        def normalise_on_scalar(i, cols):
            b = i // TILES_PER_BATCH
            nc.scalar.activation(
                out=y_sb[:, i, cols],
                in_=o_sb[:, i, cols],
                func=FUNC.Identity,
                scale=rstd[:, b : b + 1],
                bias=nmr[:, b : b + 1],
            )

        def scale_on_scalar(i, cols):
            b = i // TILES_PER_BATCH
            nc.scalar.activation(
                out=o_sb[:, i, cols], in_=y_sb[:, i, cols], func=FUNC.Identity, scale=rstd[:, b : b + 1]
            )

        def shift_and_store_on_gpsimd(i, cols):
            nc.gpsimd.tensor_tensor(
                out=y_sb[:, i, cols], in0=o_sb[:, i, cols], in1=beta_sb[:, i % TILES_PER_BATCH, cols], op=ALU.add
            )
            nc.scalar.dma_start(out=of_tile(out_view, i)[:, cols], in_=y_sb[:, i, cols])

        def gain_shift_and_store_on_gpsimd(i, cols):
            nc.gpsimd.tensor_tensor(
                out=o_sb[:, i, cols], in0=y_sb[:, i, cols], in1=gamma_sb[:, i % TILES_PER_BATCH, cols], op=ALU.mult
            )
            nc.gpsimd.tensor_tensor(
                out=y_sb[:, i, cols], in0=o_sb[:, i, cols], in1=beta_sb[:, i % TILES_PER_BATCH, cols], op=ALU.add
            )
            nc.scalar.dma_start(out=of_tile(out_view, i)[:, cols], in_=y_sb[:, i, cols])

        def shift_and_store_on_vector(i, cols):
            nc.vector.tensor_tensor(
                out=y_sb[:, i, cols], in0=o_sb[:, i, cols], in1=beta_sb[:, i % TILES_PER_BATCH, cols], op=ALU.add
            )
            store(i, cols)

        def gain_on_gpsimd(i):
            nc.gpsimd.tensor_tensor(
                out=o_sb[:, i, :], in0=y_sb[:, i, :], in1=gamma_sb[:, i % TILES_PER_BATCH, :], op=ALU.mult
            )

        def add_bias_and_residual_on_gpsimd(i, where):
            nc.gpsimd.tensor_tensor(out=where, in0=bo_sb[:, i, :], in1=x_sb[:, i, :], op=ALU.add)

        transpose(0)
        regroup(0)
        transpose(1)
        regroup(1)
        quantise(0)
        project(0)
        add_bias_and_residual(0)
        quantise(1)
        transpose(2)
        regroup(2)
        project(1)
        add_product(0)
        take_shift(0)
        sum_squares(0)
        add_bias_and_residual(1)
        quantise(2)
        transpose(3)
        regroup(3)
        project(2)
        transpose(4)
        regroup(4)
        add_product(1)
        sum_squares(1)
        add_bias_and_residual(2)
        quantise(3)
        quantise(4)
        transpose(5)
        regroup(5)
        project(3)
        transpose(6)
        regroup(6)
        add_bias_and_residual(3)
        quantise(5)
        quantise(6)
        transpose(7)
        regroup(7)
        project(4)
        quantise(7)
        first_sum = reused.tile([P, N], F32, offset=0)
        summed_at[4] = first_sum
        add_bias_and_residual_on_gpsimd(4, first_sum[:])
        add_bias_and_residual_on_gpsimd(5, o_sb[:, 5, :])
        add_bias_and_residual_on_gpsimd(6, o_sb[:, 6, :])
        add_bias_and_residual_on_gpsimd(7, o_sb[:, 7, :])
        project(5)
        add_product(2)
        sum_squares(2)
        lay_in_psum("gamma", gamma_sb, 0)
        lay_in_psum("gamma", gamma_sb, 1)
        add_product(3)
        take_negmean(0)
        sum_squares(3)
        take_rstd(0)
        take_nmr(0)
        normalise_on_scalar(3, WHOLE)
        lay_in_psum("gamma", gamma_sb, 2)
        add_product(4)
        take_shift(1)
        sum_squares(4)
        project(6)
        centre_and_gain(0)
        add_product(5)
        sum_squares(5)
        project(7)
        centre_and_gain(1)
        add_product(6)
        sum_squares(6)
        lay_in_psum("beta", beta_sb, 0)
        lay_in_psum("beta", beta_sb, 1)
        lay_in_psum("beta", beta_sb, 2)
        centre_and_gain(2)
        scale_on_scalar(2, GPSIMD_SHARE)
        add_product(7)
        sum_squares(7)
        take_negmean(1)
        take_rstd(1)
        take_nmr(1)
        normalise_on_scalar(7, WHOLE)
        scale_shift_and_store(0)
        scale_shift_and_store(1)
        scale_shift_and_store(2, VECTOR_SHARE)
        gain_shift_and_store_on_gpsimd(3, WHOLE)
        shift_and_store_on_gpsimd(2, GPSIMD_SHARE)
        gain_on_gpsimd(7)
        shift_and_store_on_gpsimd(7, FIRST_HALF)
        shift_and_store_on_gpsimd(7, SECOND_HALF)
        centre_and_gain(4)
        centre_and_gain(5)
        scale_shift_and_store(4)
        scale_shift_and_store(5)
        centre_and_gain(6)
        scale_shift_and_store(6, FIRST_HALF)
        scale_shift_and_store(6, SECOND_HALF)
